import numpy as np
import ml_dtypes


def mxq(x, axis, fmt="e4m3"):
    dtype, down = {"e4m3": (ml_dtypes.float8_e4m3fn, 7), "e5m2": (ml_dtypes.float8_e5m2, 14)}[fmt]
    v = np.moveaxis(np.asarray(x, np.float32).astype(ml_dtypes.bfloat16).astype(np.float64), axis, -1)
    blocks = v.reshape(v.shape[:-1] + (-1, 32))
    amax = np.abs(blocks).max(-1, keepdims=True)
    byte = np.maximum(np.where(amax > 0, np.frexp(amax)[1] - 1 + 127, 0) - down, 1)
    scale = np.exp2(byte - 127.0)
    codes = (blocks / scale).astype(np.float32).astype(dtype).astype(np.float64)
    return np.moveaxis((codes * scale).reshape(v.shape), -1, axis)


WIDE = False


def mx_kscale(k):
    if not WIDE:
        return np.ones(k)
    levels = np.array([10, -10, 5, -5, 0])
    a = np.random.permutation(np.resize(levels, k // 512 * 4)).reshape(k // 512, 4)
    idx = np.arange(k)
    return np.exp2(a[idx // 512, idx % 128 // 32])


BF16 = ml_dtypes.bfloat16


def bf(x):
    return np.asarray(x, np.float32).astype(BF16)


def f64(x):
    return np.asarray(x).astype(np.float64)


B, C, T, V, OUT, REL, TS = 1, 512, 128, 32, 1024, 64, 16
TP = T + TS - 1
K = V * TS


def setup_inputs():
    s = mx_kscale(K)[::TS]
    t = mx_kscale(C)
    return {'x_pad': bf(np.random.standard_normal((B, C, TP, V)) * t[None, :, None, None] * s),
            'rel': bf(np.random.standard_normal((B, C * TS, V, V)) / np.sqrt(K) / s[:, None]),
            'A': bf(np.random.standard_normal((V, V)) * 0.7 / np.sqrt(K) / s[:, None]),
            'w3': bf(np.random.standard_normal((OUT, C)) / np.sqrt(C) / t),
            'b3': bf(np.random.standard_normal(OUT) * 0.3)}


def reference(x_pad, rel, A, w3, b3):
    adj = f64(rel) + f64(A)[None, None]
    W = adj.reshape(B, C, TS, V, V).transpose(0, 1, 3, 2, 4).reshape(B, C, K, V)
    xf = f64(x_pad)
    xw = np.stack([xf[:, :, k:k + T, :] for k in range(TS)], axis=-1).reshape(B, C, T, K)
    z = mxq(xw, 3, 'e4m3') @ mxq(W, 2, 'e4m3')
    y = mxq(f64(w3), 1, 'e4m3') @ mxq(z.reshape(B, C, T * V), 1, 'e4m3')
    return (y + f64(b3)[None, :, None]).reshape(B, OUT, T, V)

@@ -1,0 +1,223 @@
+from contextlib import ExitStack
+
+import concourse.mybir as mybir
+from concourse.masks import make_identity
+
+FLOPS = 2 * 512 * 128 * 512 * 32 + 2 * 1024 * 512 * 128 * 32
+
+BF16 = mybir.dt.bfloat16
+F32 = mybir.dt.float32
+U32 = mybir.dt.uint32
+U8 = mybir.dt.uint8
+FP8X4 = mybir.dt.float8_e4m3fn_x4
+ADD = mybir.AluOpType.add
+IDENTITY = mybir.ActivationFunctionType.Identity
+
+P = 128
+PACK = 4
+C = 512
+T = 128
+V = 32
+FRAMES = 143
+OUT = 1024
+PAIRS = V // 2
+KA = 8
+PITCH = 144
+NEED = T + KA
+CHUNK = 32
+GROUP = 8
+QUAD = 4
+N_TILE = 512
+T_STEP = N_TILE // V
+
+
+def tile_gccgc_pa_t_kernel(tc, x_pad, rel, A, w3, b3, out):
+    nc = tc.nc
+
+    out_words = out.rearrange("b o t i -> (b o t i)")
+    scratch = out_words[0 : PAIRS * C * PITCH]
+    scratch_by_channel = scratch.rearrange("(jp c f) -> c jp f", jp=PAIRS, c=C)
+    scratch_rows = scratch.rearrange("(jp x) -> jp x", jp=PAIRS)
+    rel_rows = rel[0].rearrange("(x ka) (jp e) i -> ka jp x (e i)", ka=KA, e=2)
+
+    with ExitStack() as stack:
+        keep = stack.enter_context(tc.tile_pool(name="keep", bufs=1))
+        win_pool = stack.enter_context(tc.tile_pool(name="win", bufs=2))
+        rel_pool = stack.enter_context(tc.tile_pool(name="rel", bufs=3))
+        w_pool = stack.enter_context(tc.tile_pool(name="wq", bufs=2))
+        x_pool = stack.enter_context(tc.tile_pool(name="xq", bufs=3))
+        acc_psum = stack.enter_context(tc.psum_pool(name="acc", bufs=4))
+        tr_psum = stack.enter_context(tc.psum_pool(name="tr", bufs=3))
+
+        ident = keep.tile([P, P], BF16)
+        make_identity(nc, ident[:])
+
+        with tc.tile_pool(name="sort", bufs=2) as sort_pool:
+            for block in range(C // P):
+                channels = slice(block * P, (block + 1) * P)
+                x_rows = sort_pool.tile([P, FRAMES * V], BF16)
+                nc.sync.dma_start(out=x_rows[:], in_=x_pad[0, channels].rearrange("c f v -> c (f v)"))
+                sorted_rows = sort_pool.tile([P, PAIRS, PITCH], F32)
+                nc.vector.memset(sorted_rows[:, :, FRAMES:PITCH], 0.0)
+                nc.vector.tensor_copy(
+                    out=sorted_rows[:, :, 0:FRAMES],
+                    in_=x_rows[:].bitcast(F32).rearrange("c (f jp) -> c jp f", jp=PAIRS),
+                )
+                nc.sync.dma_start(out=scratch_by_channel[channels], in_=sorted_rows[:])
+
+        a_raw = keep.tile([P, 2, V], BF16)
+        for ka in range(KA):
+            nc.sync.dma_start(
+                out=a_raw[ka:P:KA].rearrange("p e i -> p (e i)"),
+                in_=A.rearrange("(jp e) i -> jp (e i)", e=2),
+            )
+        a_words = keep.tile([P, V, 2, 2], BF16)
+        for kh in range(2):
+            nc.vector.tensor_copy(out=a_words[:, :, kh, :], in_=a_raw[:].rearrange("p e i -> p i e"))
+
+        b3_rows = keep.tile([P, P], BF16)
+        nc.vector.memset(b3_rows[:], 0.0)
+        nc.sync.dma_start(out=b3_rows[0 : OUT // P, :], in_=b3.rearrange("(a o) -> a o", o=P))
+        b3_ps = tr_psum.tile([P, P], BF16, tag="tr")
+        nc.tensor.transpose(b3_ps[:], b3_rows[:], ident[:])
+        b3_cols = keep.tile([P, OUT // P], F32)
+        nc.vector.tensor_copy(out=b3_cols[:], in_=b3_ps[:, 0 : OUT // P])
+
+        w3_codes = keep.tile([P, OUT], U32, align_bytes=64)
+        w3_scales = keep.tile([P, OUT], U8, align_bytes=64)
+        with tc.tile_pool(name="w3", bufs=1) as w3_pool:
+            w3_rows = w3_pool.tile([P, OUT // P, C], BF16)
+            nc.sync.dma_start(out=w3_rows[:], in_=w3.rearrange("(a p) c -> p a c", p=P))
+            w3_in = w3_pool.tile([P, OUT, PACK], BF16, align_bytes=64)
+            for two in range(OUT // P // 2):
+                w3_ps = tr_psum.tile([P, 2 * PACK, P], BF16, tag="tr")
+                for a in range(2):
+                    for r in range(PACK):
+                        nc.tensor.transpose(
+                            w3_ps[:, a * PACK + r, :], w3_rows[:, 2 * two + a, r * P : (r + 1) * P], ident[:]
+                        )
+                nc.scalar.copy(
+                    out=w3_in[:, 2 * two * P : (2 * two + 2) * P, :].rearrange("p (a o) r -> p a o r", a=2),
+                    in_=w3_ps[:].rearrange("p (a r) o -> p a o r", a=2),
+                )
+            nc.vector.quantize_mx(
+                out=w3_codes[:].bitcast(FP8X4),
+                scales=w3_scales[:],
+                in_=w3_in[:].rearrange("p o r -> p (o r)"),
+            )
+
+        late = stack.enter_context(tc.tile_pool(name="late", bufs=1))
+        z_pool = stack.enter_context(tc.tile_pool(name="zq", bufs=2))
+        y_pool = stack.enter_context(tc.tile_pool(name="y", bufs=4))
+
+        z_sb = keep.tile([P, V, C], BF16)
+        z_t = late.tile([P, PACK, T, V], BF16)
+
+        run = (CHUNK - 1) * PITCH + NEED
+        for chunk in range(C // CHUNK):
+            c0 = chunk * CHUNK
+
+            frames = win_pool.tile([P, CHUNK * PITCH], F32)
+            for ka in range(KA):
+                first = c0 * PITCH + ka
+                nc.scalar.dma_start(out=frames[ka:P:KA, 0:run], in_=scratch_rows[:, first : first + run])
+            blocks = frames[:].rearrange("p (c u b) -> p c u b", c=CHUNK, b=KA)
+
+            raw = rel_pool.tile([P, CHUNK, PACK, V], BF16)
+            for ka in range(KA):
+                nc.sync.dma_start(
+                    out=raw[ka:P:KA].rearrange("p c (kh e) i -> p (c kh) (e i)", e=2),
+                    in_=rel_rows[ka, :, 2 * c0 : 2 * (c0 + CHUNK), :],
+                )
+            w_in = w_pool.tile([P, CHUNK, V, PACK], BF16, align_bytes=64)
+            nc.vector.tensor_tensor(
+                out=w_in[:],
+                in0=raw[:].rearrange("p c r i -> p c i r"),
+                in1=a_words[:].rearrange("p i kh e -> p i (kh e)").unsqueeze(1).to_broadcast([P, CHUNK, V, PACK]),
+                op=ADD,
+            )
+            w_codes = w_pool.tile([P, CHUNK * V], U32, align_bytes=64)
+            w_scales = w_pool.tile([P, CHUNK * V], U8, align_bytes=64)
+            nc.vector.quantize_mx(
+                out=w_codes[:].bitcast(FP8X4),
+                scales=w_scales[:],
+                in_=w_in[:].rearrange("p c i r -> p (c i r)"),
+            )
+
+            for group in range(CHUNK // GROUP):
+                g0 = group * GROUP
+                x_in = x_pool.tile([P, GROUP * T * PACK], BF16, align_bytes=64)
+                words = x_in[:].bitcast(F32).rearrange(
+                    "p (c a odd b kh) -> p c a odd b kh", c=GROUP, odd=2, b=KA, kh=2
+                )
+                for odd in range(2):
+                    nc.scalar.copy(
+                        out=words[:, :, :, odd],
+                        in_=blocks[:, g0 : g0 + GROUP, odd : odd + T // KA, :].rearrange(
+                            "p c (a kh) b -> p c a b kh", kh=2
+                        ),
+                    )
+                x_codes = x_pool.tile([P, GROUP * T], U32, align_bytes=64)
+                x_scales = x_pool.tile([P, GROUP * T], U8, align_bytes=64)
+                nc.vector.quantize_mx(out=x_codes[:].bitcast(FP8X4), scales=x_scales[:], in_=x_in[:])
+
+                for quad in range(GROUP // QUAD):
+                    q0 = g0 + quad * QUAD
+                    w_cols = slice(q0 * V, (q0 + QUAD) * V)
+                    acc = acc_psum.tile([P, QUAD * QUAD * V], F32, tag="acc")
+                    for q in range(QUAD):
+                        t_cols = slice((quad * QUAD + q) * T, (quad * QUAD + q + 1) * T)
+                        nc.tensor.matmul_mx(
+                            out=acc[:, q * QUAD * V : (q + 1) * QUAD * V],
+                            lhsT=x_codes[:, t_cols].bitcast(FP8X4),
+                            lhsT_scale=x_scales[:, t_cols],
+                            rhs=w_codes[:, w_cols].bitcast(FP8X4),
+                            rhs_scale=w_scales[:, w_cols],
+                            start=True,
+                            stop=True,
+                        )
+                    own = acc[:].rearrange("p (blk i) -> p blk i", i=V)[:, 0 : QUAD * QUAD : QUAD + 1, :]
+                    nc.scalar.copy(
+                        out=z_sb[:, :, c0 + q0 : c0 + q0 + QUAD],
+                        in_=own.rearrange("p q i -> p i q"),
+                    )
+
+            if (c0 + CHUNK) % P == 0:
+                r = c0 // P
+                for i0 in range(0, V, 8):
+                    z_ps = tr_psum.tile([P, 8, T], BF16, tag="tr")
+                    for i in range(8):
+                        nc.tensor.transpose(z_ps[:, i, :], z_sb[:, i0 + i, r * P : (r + 1) * P], ident[:])
+                    nc.vector.tensor_copy(
+                        out=z_t[:, r, :, i0 : i0 + 8], in_=z_ps[:].rearrange("p i t -> p t i")
+                    )
+
+        for step in range(T // T_STEP):
+            t_rows = slice(step * T_STEP, (step + 1) * T_STEP)
+            z_in = z_pool.tile([P, N_TILE, PACK], BF16, align_bytes=64)
+            nc.vector.tensor_copy(out=z_in[:], in_=z_t[:, :, t_rows, :].rearrange("p r t i -> p (t i) r"))
+            z_codes = z_pool.tile([P, N_TILE], U32, align_bytes=64)
+            z_scales = z_pool.tile([P, N_TILE], U8, align_bytes=64)
+            nc.vector.quantize_mx(
+                out=z_codes[:].bitcast(FP8X4),
+                scales=z_scales[:],
+                in_=z_in[:].rearrange("p n r -> p (n r)"),
+            )
+            for a in range(OUT // P):
+                o_cols = slice(a * P, (a + 1) * P)
+                y_ps = acc_psum.tile([P, N_TILE], F32, tag="acc")
+                nc.tensor.matmul_mx(
+                    out=y_ps[:],
+                    lhsT=w3_codes[:, o_cols].bitcast(FP8X4),
+                    lhsT_scale=w3_scales[:, o_cols],
+                    rhs=z_codes[:].bitcast(FP8X4),
+                    rhs_scale=z_scales[:],
+                    start=True,
+                    stop=True,
+                )
+                y = y_pool.tile([P, N_TILE], F32)
+                if a % 2 == 0:
+                    nc.scalar.activation(out=y[:], in_=y_ps[:], func=IDENTITY, bias=b3_cols[:, a : a + 1])
+                else:
+                    nc.vector.tensor_scalar_add(out=y[:], in0=y_ps[:], scalar1=b3_cols[:, a : a + 1])
+                nc.sync.dma_start(out=out[0, o_cols, t_rows, :].rearrange("o t i -> o (t i)"), in_=y[:])

@@ -24,6 +24,7 @@ PAIRS = V // 2
 KA = 8
 PITCH = 144
 NEED = T + KA
+BLOCK = 128
 CHUNK = 32
 GROUP = 8
 QUAD = 4
@@ -33,61 +34,173 @@ T_STEP = N_TILE // V
 
 def tile_gccgc_pa_t_kernel(tc, x_pad, rel, A, w3, b3, out):
     nc = tc.nc
+    n_groups = C // GROUP
+    groups_in_chunk = CHUNK // GROUP
+    groups_in_block = BLOCK // GROUP
+    n_chunks = C // CHUNK
+    run = (CHUNK - 1) * PITCH + NEED
 
     out_words = out.rearrange("b o t i -> (b o t i)")
-    scratch = out_words[0 : PAIRS * C * PITCH]
-    scratch_by_channel = scratch.rearrange("(jp c f) -> c jp f", jp=PAIRS, c=C)
-    scratch_rows = scratch.rearrange("(jp x) -> jp x", jp=PAIRS)
+    scratch = out_words[0 : PAIRS * C * PITCH].rearrange("(blk x) -> blk x", blk=C // BLOCK)
     rel_rows = rel[0].rearrange("(x ka) (jp e) i -> ka jp x (e i)", ka=KA, e=2)
 
     with ExitStack() as stack:
         keep = stack.enter_context(tc.tile_pool(name="keep", bufs=1))
+        sort_pool = stack.enter_context(tc.tile_pool(name="sort", bufs=1))
         win_pool = stack.enter_context(tc.tile_pool(name="win", bufs=2))
-        rel_pool = stack.enter_context(tc.tile_pool(name="rel", bufs=3))
+        rel_pool = stack.enter_context(tc.tile_pool(name="rel", bufs=2))
         w_pool = stack.enter_context(tc.tile_pool(name="wq", bufs=2))
         x_pool = stack.enter_context(tc.tile_pool(name="xq", bufs=3))
         acc_psum = stack.enter_context(tc.psum_pool(name="acc", bufs=4))
         tr_psum = stack.enter_context(tc.psum_pool(name="tr", bufs=3))
+        stack.enter_context(tc.manual_schedule())
 
+        x_rows_of = {}
+        frames_of = {}
+        raw_of = {}
+        w_codes_of = {}
+        w_scales_of = {}
+        x_in_of = {}
+        x_codes_of = {}
+        x_scales_of = {}
+        acc_of = {}
+
+        def load_block(block):
+            x_rows_of[block] = sort_pool.tile([P, FRAMES * V], BF16, name="x_rows")
+            nc.sync.dma_start(
+                out=x_rows_of[block][:],
+                in_=x_pad[0, block * BLOCK : (block + 1) * BLOCK].rearrange("c f v -> c (f v)"),
+            )
+
+        def sort_block(block):
+            sorted_rows = sort_pool.tile([P, PAIRS, PITCH], F32)
+            nc.vector.memset(sorted_rows[:, :, FRAMES:PITCH], 0.0)
+            nc.vector.tensor_copy(
+                out=sorted_rows[:, :, 0:FRAMES],
+                in_=x_rows_of[block][:].bitcast(F32).rearrange("c (f jp) -> c jp f", jp=PAIRS),
+            )
+            nc.sync.dma_start(
+                out=scratch[block].rearrange("(jp c f) -> c jp f", jp=PAIRS, c=BLOCK), in_=sorted_rows[:]
+            )
+
+        def load_frames(chunk):
+            frames_of[chunk] = win_pool.tile([P, CHUNK * PITCH], F32, name="frames")
+            rows = scratch[chunk * CHUNK // BLOCK].rearrange("(jp x) -> jp x", jp=PAIRS)
+            for ka in range(KA):
+                first = (chunk * CHUNK % BLOCK) * PITCH + ka
+                nc.sync.dma_start(out=frames_of[chunk][ka:P:KA, 0:run], in_=rows[:, first : first + run])
+
+        def load_rel(chunk):
+            raw_of[chunk] = rel_pool.tile([P, CHUNK, PACK, V], BF16, name="raw")
+            for ka in range(KA):
+                nc.sync.dma_start(
+                    out=raw_of[chunk][ka:P:KA].rearrange("p c (kh e) i -> p (c kh) (e i)", e=2),
+                    in_=rel_rows[ka, :, 2 * chunk * CHUNK : 2 * (chunk + 1) * CHUNK, :],
+                )
+
+        def weights(group):
+            chunk = group // groups_in_chunk
+            g0 = group % groups_in_chunk * GROUP
+            if g0 == 0:
+                w_codes_of[chunk] = w_pool.tile([P, CHUNK * V], U32, align_bytes=64, name="w_codes")
+                w_scales_of[chunk] = w_pool.tile([P, CHUNK * V], U8, align_bytes=64, name="w_scales")
+            w_in = w_pool.tile([P, GROUP, V, PACK], BF16, align_bytes=64)
+            nc.vector.tensor_tensor(
+                out=w_in[:],
+                in0=raw_of[chunk][:, g0 : g0 + GROUP].rearrange("p c r i -> p c i r"),
+                in1=a_words[:].rearrange("p i kh e -> p i (kh e)").unsqueeze(1).to_broadcast([P, GROUP, V, PACK]),
+                op=ADD,
+            )
+            cols = slice(g0 * V, (g0 + GROUP) * V)
+            nc.vector.quantize_mx(
+                out=w_codes_of[chunk][:, cols].bitcast(FP8X4),
+                scales=w_scales_of[chunk][:, cols],
+                in_=w_in[:].rearrange("p c i r -> p (c i r)"),
+            )
+
+        def windows(group):
+            g0 = group % groups_in_chunk * GROUP
+            blocks = frames_of[group // groups_in_chunk][:].rearrange("p (c u b) -> p c u b", c=CHUNK, b=KA)
+            x_in_of[group] = x_pool.tile([P, GROUP * T * PACK], BF16, align_bytes=64, name="x_in")
+            words = x_in_of[group][:].bitcast(F32).rearrange(
+                "p (c a odd b kh) -> p c a odd b kh", c=GROUP, odd=2, b=KA, kh=2
+            )
+            for odd in range(2):
+                nc.scalar.copy(
+                    out=words[:, :, :, odd],
+                    in_=blocks[:, g0 : g0 + GROUP, odd : odd + T // KA, :].rearrange(
+                        "p c (a kh) b -> p c a b kh", kh=2
+                    ),
+                )
+
+        def multiply(group):
+            x_codes = x_pool.tile([P, GROUP * T], U32, align_bytes=64)
+            x_scales = x_pool.tile([P, GROUP * T], U8, align_bytes=64)
+            nc.vector.quantize_mx(out=x_codes[:].bitcast(FP8X4), scales=x_scales[:], in_=x_in_of[group][:])
+            chunk = group // groups_in_chunk
+            for quad in range(GROUP // QUAD):
+                q0 = group % groups_in_chunk * GROUP + quad * QUAD
+                w_cols = slice(q0 * V, (q0 + QUAD) * V)
+                acc = acc_psum.tile([P, QUAD * QUAD * V], F32, tag="acc", name="acc")
+                acc_of[(group, quad)] = acc
+                for q in range(QUAD):
+                    t_cols = slice((quad * QUAD + q) * T, (quad * QUAD + q + 1) * T)
+                    nc.tensor.matmul_mx(
+                        out=acc[:, q * QUAD * V : (q + 1) * QUAD * V],
+                        lhsT=x_codes[:, t_cols].bitcast(FP8X4),
+                        lhsT_scale=x_scales[:, t_cols],
+                        rhs=w_codes_of[chunk][:, w_cols].bitcast(FP8X4),
+                        rhs_scale=w_scales_of[chunk][:, w_cols],
+                        start=True,
+                        stop=True,
+                    )
+
+        def collect(group):
+            for quad in range(GROUP // QUAD):
+                c0 = group * GROUP + quad * QUAD
+                own = acc_of[(group, quad)][:].rearrange("p (blk i) -> p blk i", i=V)[:, 0 : QUAD * QUAD : QUAD + 1, :]
+                if group // 2 % 2 == 0:
+                    nc.scalar.copy(out=z_sb[:, :, c0 : c0 + QUAD], in_=own.rearrange("p q i -> p i q"))
+                else:
+                    nc.vector.tensor_copy(out=z_sb[:, :, c0 : c0 + QUAD], in_=own.rearrange("p q i -> p i q"))
+
+        def turn(r):
+            for i0 in range(0, V, 8):
+                z_ps = tr_psum.tile([P, 8, T], BF16, tag="tr")
+                for i in range(8):
+                    nc.tensor.transpose(z_ps[:, i, :], z_sb[:, i0 + i, r * P : (r + 1) * P], ident[:])
+                if i0 < V // 2:
+                    nc.scalar.copy(out=z_t[:, r, :, i0 : i0 + 8], in_=z_ps[:].rearrange("p i t -> p t i"))
+                else:
+                    nc.vector.tensor_copy(out=z_t[:, r, :, i0 : i0 + 8], in_=z_ps[:].rearrange("p i t -> p t i"))
+
+        load_block(0)
         ident = keep.tile([P, P], BF16)
         make_identity(nc, ident[:])
-
-        with tc.tile_pool(name="sort", bufs=2) as sort_pool:
-            for block in range(C // P):
-                channels = slice(block * P, (block + 1) * P)
-                x_rows = sort_pool.tile([P, FRAMES * V], BF16)
-                nc.sync.dma_start(out=x_rows[:], in_=x_pad[0, channels].rearrange("c f v -> c (f v)"))
-                sorted_rows = sort_pool.tile([P, PAIRS, PITCH], F32)
-                nc.vector.memset(sorted_rows[:, :, FRAMES:PITCH], 0.0)
-                nc.vector.tensor_copy(
-                    out=sorted_rows[:, :, 0:FRAMES],
-                    in_=x_rows[:].bitcast(F32).rearrange("c (f jp) -> c jp f", jp=PAIRS),
-                )
-                nc.sync.dma_start(out=scratch_by_channel[channels], in_=sorted_rows[:])
-
         a_raw = keep.tile([P, 2, V], BF16)
         for ka in range(KA):
             nc.sync.dma_start(
                 out=a_raw[ka:P:KA].rearrange("p e i -> p (e i)"),
                 in_=A.rearrange("(jp e) i -> jp (e i)", e=2),
             )
-        a_words = keep.tile([P, V, 2, 2], BF16)
-        for kh in range(2):
-            nc.vector.tensor_copy(out=a_words[:, :, kh, :], in_=a_raw[:].rearrange("p e i -> p i e"))
-
         b3_rows = keep.tile([P, P], BF16)
         nc.vector.memset(b3_rows[:], 0.0)
         nc.sync.dma_start(out=b3_rows[0 : OUT // P, :], in_=b3.rearrange("(a o) -> a o", o=P))
-        b3_ps = tr_psum.tile([P, P], BF16, tag="tr")
-        nc.tensor.transpose(b3_ps[:], b3_rows[:], ident[:])
-        b3_cols = keep.tile([P, OUT // P], F32)
-        nc.vector.tensor_copy(out=b3_cols[:], in_=b3_ps[:, 0 : OUT // P])
-
         w3_codes = keep.tile([P, OUT], U32, align_bytes=64)
         w3_scales = keep.tile([P, OUT], U8, align_bytes=64)
         with tc.tile_pool(name="w3", bufs=1) as w3_pool:
             w3_rows = w3_pool.tile([P, OUT // P, C], BF16)
             nc.sync.dma_start(out=w3_rows[:], in_=w3.rearrange("(a p) c -> p a c", p=P))
+            load_rel(0)
+            sort_block(0)
+            load_frames(0)
+            load_rel(1)
+
+            b3_ps = tr_psum.tile([P, P], BF16, tag="tr")
+            nc.tensor.transpose(b3_ps[:], b3_rows[:], ident[:])
+            b3_cols = keep.tile([P, OUT // P], F32)
+            nc.vector.tensor_copy(out=b3_cols[:], in_=b3_ps[:, 0 : OUT // P])
+
             w3_in = w3_pool.tile([P, OUT, PACK], BF16, align_bytes=64)
             for two in range(OUT // P // 2):
                 w3_ps = tr_psum.tile([P, 2 * PACK, P], BF16, tag="tr")
@@ -106,103 +219,61 @@ def tile_gccgc_pa_t_kernel(tc, x_pad, rel, A, w3, b3, out):
                 in_=w3_in[:].rearrange("p o r -> p (o r)"),
             )
 
+        a_words = keep.tile([P, V, 2, 2], BF16)
+        for kh in range(2):
+            nc.vector.tensor_copy(out=a_words[:, :, kh, :], in_=a_raw[:].rearrange("p e i -> p i e"))
+        for group in range(groups_in_chunk):
+            weights(group)
+
         late = stack.enter_context(tc.tile_pool(name="late", bufs=1))
         z_pool = stack.enter_context(tc.tile_pool(name="zq", bufs=2))
         y_pool = stack.enter_context(tc.tile_pool(name="y", bufs=4))
-
         z_sb = keep.tile([P, V, C], BF16)
         z_t = late.tile([P, PACK, T, V], BF16)
 
-        run = (CHUNK - 1) * PITCH + NEED
-        for chunk in range(C // CHUNK):
-            c0 = chunk * CHUNK
+        for s in range(n_groups + 3):
+            if s % groups_in_chunk == 0:
+                chunk = s // groups_in_chunk
+                if chunk + 1 < n_chunks:
+                    load_frames(chunk + 1)
+                if chunk + 2 < n_chunks:
+                    load_rel(chunk + 2)
+            if s % groups_in_block == 0 and s + groups_in_block < n_groups:
+                load_block(s // groups_in_block + 1)
+            if s < n_groups:
+                windows(s)
+            if 1 <= s <= n_groups:
+                multiply(s - 1)
+            if 2 <= s <= n_groups + 1:
+                collect(s - 2)
+            if s + groups_in_chunk < n_groups:
+                weights(s + groups_in_chunk)
+            if s % groups_in_block == groups_in_chunk and s + groups_in_block < n_groups:
+                sort_block(s // groups_in_block + 1)
+            if s >= 3 and (s - 2) % groups_in_block == 0:
+                turn((s - 3) // groups_in_block)
 
-            frames = win_pool.tile([P, CHUNK * PITCH], F32)
-            for ka in range(KA):
-                first = c0 * PITCH + ka
-                nc.scalar.dma_start(out=frames[ka:P:KA, 0:run], in_=scratch_rows[:, first : first + run])
-            blocks = frames[:].rearrange("p (c u b) -> p c u b", c=CHUNK, b=KA)
+        z_codes_of = {}
+        z_scales_of = {}
 
-            raw = rel_pool.tile([P, CHUNK, PACK, V], BF16)
-            for ka in range(KA):
-                nc.sync.dma_start(
-                    out=raw[ka:P:KA].rearrange("p c (kh e) i -> p (c kh) (e i)", e=2),
-                    in_=rel_rows[ka, :, 2 * c0 : 2 * (c0 + CHUNK), :],
-                )
-            w_in = w_pool.tile([P, CHUNK, V, PACK], BF16, align_bytes=64)
-            nc.vector.tensor_tensor(
-                out=w_in[:],
-                in0=raw[:].rearrange("p c r i -> p c i r"),
-                in1=a_words[:].rearrange("p i kh e -> p i (kh e)").unsqueeze(1).to_broadcast([P, CHUNK, V, PACK]),
-                op=ADD,
-            )
-            w_codes = w_pool.tile([P, CHUNK * V], U32, align_bytes=64)
-            w_scales = w_pool.tile([P, CHUNK * V], U8, align_bytes=64)
-            nc.vector.quantize_mx(
-                out=w_codes[:].bitcast(FP8X4),
-                scales=w_scales[:],
-                in_=w_in[:].rearrange("p c i r -> p (c i r)"),
-            )
-
-            for group in range(CHUNK // GROUP):
-                g0 = group * GROUP
-                x_in = x_pool.tile([P, GROUP * T * PACK], BF16, align_bytes=64)
-                words = x_in[:].bitcast(F32).rearrange(
-                    "p (c a odd b kh) -> p c a odd b kh", c=GROUP, odd=2, b=KA, kh=2
-                )
-                for odd in range(2):
-                    nc.scalar.copy(
-                        out=words[:, :, :, odd],
-                        in_=blocks[:, g0 : g0 + GROUP, odd : odd + T // KA, :].rearrange(
-                            "p c (a kh) b -> p c a b kh", kh=2
-                        ),
-                    )
-                x_codes = x_pool.tile([P, GROUP * T], U32, align_bytes=64)
-                x_scales = x_pool.tile([P, GROUP * T], U8, align_bytes=64)
-                nc.vector.quantize_mx(out=x_codes[:].bitcast(FP8X4), scales=x_scales[:], in_=x_in[:])
-
-                for quad in range(GROUP // QUAD):
-                    q0 = g0 + quad * QUAD
-                    w_cols = slice(q0 * V, (q0 + QUAD) * V)
-                    acc = acc_psum.tile([P, QUAD * QUAD * V], F32, tag="acc")
-                    for q in range(QUAD):
-                        t_cols = slice((quad * QUAD + q) * T, (quad * QUAD + q + 1) * T)
-                        nc.tensor.matmul_mx(
-                            out=acc[:, q * QUAD * V : (q + 1) * QUAD * V],
-                            lhsT=x_codes[:, t_cols].bitcast(FP8X4),
-                            lhsT_scale=x_scales[:, t_cols],
-                            rhs=w_codes[:, w_cols].bitcast(FP8X4),
-                            rhs_scale=w_scales[:, w_cols],
-                            start=True,
-                            stop=True,
-                        )
-                    own = acc[:].rearrange("p (blk i) -> p blk i", i=V)[:, 0 : QUAD * QUAD : QUAD + 1, :]
-                    nc.scalar.copy(
-                        out=z_sb[:, :, c0 + q0 : c0 + q0 + QUAD],
-                        in_=own.rearrange("p q i -> p i q"),
-                    )
-
-            if (c0 + CHUNK) % P == 0:
-                r = c0 // P
-                for i0 in range(0, V, 8):
-                    z_ps = tr_psum.tile([P, 8, T], BF16, tag="tr")
-                    for i in range(8):
-                        nc.tensor.transpose(z_ps[:, i, :], z_sb[:, i0 + i, r * P : (r + 1) * P], ident[:])
-                    nc.vector.tensor_copy(
-                        out=z_t[:, r, :, i0 : i0 + 8], in_=z_ps[:].rearrange("p i t -> p t i")
-                    )
-
-        for step in range(T // T_STEP):
+        def quantise_z(step):
             t_rows = slice(step * T_STEP, (step + 1) * T_STEP)
             z_in = z_pool.tile([P, N_TILE, PACK], BF16, align_bytes=64)
             nc.vector.tensor_copy(out=z_in[:], in_=z_t[:, :, t_rows, :].rearrange("p r t i -> p (t i) r"))
-            z_codes = z_pool.tile([P, N_TILE], U32, align_bytes=64)
-            z_scales = z_pool.tile([P, N_TILE], U8, align_bytes=64)
+            z_codes_of[step] = z_pool.tile([P, N_TILE], U32, align_bytes=64, name="z_codes")
+            z_scales_of[step] = z_pool.tile([P, N_TILE], U8, align_bytes=64, name="z_scales")
             nc.vector.quantize_mx(
-                out=z_codes[:].bitcast(FP8X4),
-                scales=z_scales[:],
+                out=z_codes_of[step][:].bitcast(FP8X4),
+                scales=z_scales_of[step][:],
                 in_=z_in[:].rearrange("p n r -> p (n r)"),
             )
+
+        n_steps = T // T_STEP
+        quantise_z(0)
+        for step in range(n_steps):
+            t_rows = slice(step * T_STEP, (step + 1) * T_STEP)
+            if step + 1 < n_steps:
+                quantise_z(step + 1)
             for a in range(OUT // P):
                 o_cols = slice(a * P, (a + 1) * P)
                 y_ps = acc_psum.tile([P, N_TILE], F32, tag="acc")
@@ -210,14 +281,14 @@ def tile_gccgc_pa_t_kernel(tc, x_pad, rel, A, w3, b3, out):
                     out=y_ps[:],
                     lhsT=w3_codes[:, o_cols].bitcast(FP8X4),
                     lhsT_scale=w3_scales[:, o_cols],
-                    rhs=z_codes[:].bitcast(FP8X4),
-                    rhs_scale=z_scales[:],
+                    rhs=z_codes_of[step][:].bitcast(FP8X4),
+                    rhs_scale=z_scales_of[step][:],
                     start=True,
                     stop=True,
                 )
                 y = y_pool.tile([P, N_TILE], F32)
-                if a % 2 == 0:
-                    nc.scalar.activation(out=y[:], in_=y_ps[:], func=IDENTITY, bias=b3_cols[:, a : a + 1])
-                else:
+                if a % 4 == 3:
                     nc.vector.tensor_scalar_add(out=y[:], in0=y_ps[:], scalar1=b3_cols[:, a : a + 1])
+                else:
+                    nc.scalar.activation(out=y[:], in_=y_ps[:], func=IDENTITY, bias=b3_cols[:, a : a + 1])
                 nc.sync.dma_start(out=out[0, o_cols, t_rows, :].rearrange("o t i -> o (t i)"), in_=y[:])

@@ -24,6 +24,8 @@ PAIRS = V // 2
 KA = 8
 PITCH = 144
 NEED = T + KA
+COPIES = 2
+LOADS = KA // COPIES
 BLOCK = 128
 CHUNK = 32
 GROUP = 8
@@ -41,7 +43,7 @@ def tile_gccgc_pa_t_kernel(tc, x_pad, rel, A, w3, b3, out):
     run = (CHUNK - 1) * PITCH + NEED
 
     out_words = out.rearrange("b o t i -> (b o t i)")
-    scratch = out_words[0 : PAIRS * C * PITCH].rearrange("(blk x) -> blk x", blk=C // BLOCK)
+    scratch = out_words[0 : PAIRS * COPIES * C * PITCH].rearrange("(blk x) -> blk x", blk=C // BLOCK)
     rel_rows = rel[0].rearrange("(x ka) (jp e) i -> ka jp x (e i)", ka=KA, e=2)
 
     with ExitStack() as stack:
@@ -73,22 +75,22 @@ def tile_gccgc_pa_t_kernel(tc, x_pad, rel, A, w3, b3, out):
             )
 
         def sort_block(block):
-            sorted_rows = sort_pool.tile([P, PAIRS, PITCH], F32)
-            nc.vector.memset(sorted_rows[:, :, FRAMES:PITCH], 0.0)
+            sorted_rows = sort_pool.tile([P, PAIRS, PITCH + LOADS], F32)
+            nc.vector.memset(sorted_rows[:, :, FRAMES : PITCH + LOADS], 0.0)
             nc.vector.tensor_copy(
                 out=sorted_rows[:, :, 0:FRAMES],
                 in_=x_rows_of[block][:].bitcast(F32).rearrange("c (f jp) -> c jp f", jp=PAIRS),
             )
-            nc.sync.dma_start(
-                out=scratch[block].rearrange("(jp c f) -> c jp f", jp=PAIRS, c=BLOCK), in_=sorted_rows[:]
-            )
+            both = scratch[block].rearrange("(jp s c f) -> s c jp f", jp=PAIRS, s=COPIES, c=BLOCK)
+            for s in range(COPIES):
+                nc.sync.dma_start(out=both[s], in_=sorted_rows[:, :, LOADS * s : LOADS * s + PITCH])
 
         def load_frames(chunk):
             frames_of[chunk] = win_pool.tile([P, CHUNK * PITCH], F32, name="frames")
-            rows = scratch[chunk * CHUNK // BLOCK].rearrange("(jp x) -> jp x", jp=PAIRS)
-            for ka in range(KA):
-                first = (chunk * CHUNK % BLOCK) * PITCH + ka
-                nc.sync.dma_start(out=frames_of[chunk][ka:P:KA, 0:run], in_=rows[:, first : first + run])
+            rows = scratch[chunk * CHUNK // BLOCK].rearrange("(row x) -> row x", row=PAIRS * COPIES)
+            for lo in range(LOADS):
+                first = (chunk * CHUNK % BLOCK) * PITCH + lo
+                nc.sync.dma_start(out=frames_of[chunk][lo:P:LOADS, 0:run], in_=rows[:, first : first + run])
 
         def load_rel(chunk):
             raw_of[chunk] = rel_pool.tile([P, CHUNK, PACK, V], BF16, name="raw")

@@ -94,11 +94,12 @@ def tile_gccgc_pa_t_kernel(tc, x_pad, rel, A, w3, b3, out):
 
         def load_rel(chunk):
             raw_of[chunk] = rel_pool.tile([P, CHUNK, PACK, V], BF16, name="raw")
-            for ka in range(KA):
-                nc.sync.dma_start(
-                    out=raw_of[chunk][ka:P:KA].rearrange("p c (kh e) i -> p (c kh) (e i)", e=2),
-                    in_=rel_rows[ka, :, 2 * chunk * CHUNK : 2 * (chunk + 1) * CHUNK, :],
-                )
+            for lo in range(LOADS):
+                for queue, ka in ((nc.sync, lo), (nc.gpsimd, lo + LOADS)):
+                    queue.dma_start(
+                        out=raw_of[chunk][ka:P:KA].rearrange("p c (kh e) i -> p (c kh) (e i)", e=2),
+                        in_=rel_rows[ka, :, 2 * chunk * CHUNK : 2 * (chunk + 1) * CHUNK, :],
+                    )
 
         def weights(group):
             chunk = group // groups_in_chunk

@@ -28,6 +28,7 @@ COPIES = 2
 LOADS = KA // COPIES
 BLOCK = 128
 CHUNK = 32
+REL_CHUNK = 64
 GROUP = 8
 QUAD = 4
 N_TILE = 512
@@ -92,25 +93,25 @@ def tile_gccgc_pa_t_kernel(tc, x_pad, rel, A, w3, b3, out):
                 first = (chunk * CHUNK % BLOCK) * PITCH + lo
                 nc.sync.dma_start(out=frames_of[chunk][lo:P:LOADS, 0:run], in_=rows[:, first : first + run])
 
-        def load_rel(chunk):
-            raw_of[chunk] = rel_pool.tile([P, CHUNK, PACK, V], BF16, name="raw")
-            for lo in range(LOADS):
-                for queue, ka in ((nc.sync, lo), (nc.gpsimd, lo + LOADS)):
-                    queue.dma_start(
-                        out=raw_of[chunk][ka:P:KA].rearrange("p c (kh e) i -> p (c kh) (e i)", e=2),
-                        in_=rel_rows[ka, :, 2 * chunk * CHUNK : 2 * (chunk + 1) * CHUNK, :],
-                    )
+        def load_rel(part):
+            raw_of[part] = rel_pool.tile([P, REL_CHUNK, PACK, V], BF16, name="raw")
+            for ka in range(KA):
+                nc.sync.dma_start(
+                    out=raw_of[part][ka:P:KA].rearrange("p c (kh e) i -> p (c kh) (e i)", e=2),
+                    in_=rel_rows[ka, :, 2 * part * REL_CHUNK : 2 * (part + 1) * REL_CHUNK, :],
+                )
 
         def weights(group):
             chunk = group // groups_in_chunk
             g0 = group % groups_in_chunk * GROUP
+            r0 = group * GROUP % REL_CHUNK
             if g0 == 0:
                 w_codes_of[chunk] = w_pool.tile([P, CHUNK * V], U32, align_bytes=64, name="w_codes")
                 w_scales_of[chunk] = w_pool.tile([P, CHUNK * V], U8, align_bytes=64, name="w_scales")
             w_in = w_pool.tile([P, GROUP, V, PACK], BF16, align_bytes=64)
             nc.vector.tensor_tensor(
                 out=w_in[:],
-                in0=raw_of[chunk][:, g0 : g0 + GROUP].rearrange("p c r i -> p c i r"),
+                in0=raw_of[group * GROUP // REL_CHUNK][:, r0 : r0 + GROUP].rearrange("p c r i -> p c i r"),
                 in1=a_words[:].rearrange("p i kh e -> p i (kh e)").unsqueeze(1).to_broadcast([P, GROUP, V, PACK]),
                 op=ADD,
             )
@@ -239,8 +240,8 @@ def tile_gccgc_pa_t_kernel(tc, x_pad, rel, A, w3, b3, out):
                 chunk = s // groups_in_chunk
                 if chunk + 1 < n_chunks:
                     load_frames(chunk + 1)
-                if chunk + 2 < n_chunks:
-                    load_rel(chunk + 2)
+                if chunk % 2 == 1 and (chunk + 3) // 2 < C // REL_CHUNK:
+                    load_rel((chunk + 3) // 2)
             if s % groups_in_block == 0 and s + groups_in_block < n_groups:
                 load_block(s // groups_in_block + 1)
             if s < n_groups:

@@ -91,15 +91,16 @@ def tile_gccgc_pa_t_kernel(tc, x_pad, rel, A, w3, b3, out):
             rows = scratch[chunk * CHUNK // BLOCK].rearrange("(row x) -> row x", row=PAIRS * COPIES)
             for lo in range(LOADS):
                 first = (chunk * CHUNK % BLOCK) * PITCH + lo
-                nc.sync.dma_start(out=frames_of[chunk][lo:P:LOADS, 0:run], in_=rows[:, first : first + run])
+                nc.scalar.dma_start(out=frames_of[chunk][lo:P:LOADS, 0:run], in_=rows[:, first : first + run])
 
         def load_rel(part):
             raw_of[part] = rel_pool.tile([P, REL_CHUNK, PACK, V], BF16, name="raw")
-            for ka in range(KA):
-                nc.sync.dma_start(
-                    out=raw_of[part][ka:P:KA].rearrange("p c (kh e) i -> p (c kh) (e i)", e=2),
-                    in_=rel_rows[ka, :, 2 * part * REL_CHUNK : 2 * (part + 1) * REL_CHUNK, :],
-                )
+            for lo in range(LOADS):
+                for queue, ka in ((nc.sync, lo), (nc.gpsimd, lo + LOADS)):
+                    queue.dma_start(
+                        out=raw_of[part][ka:P:KA].rearrange("p c (kh e) i -> p (c kh) (e i)", e=2),
+                        in_=rel_rows[ka, :, 2 * part * REL_CHUNK : 2 * (part + 1) * REL_CHUNK, :],
+                    )
 
         def weights(group):
             chunk = group // groups_in_chunk

from contextlib import ExitStack

import concourse.mybir as mybir
from concourse.masks import make_identity

FLOPS = 2 * 512 * 128 * 512 * 32 + 2 * 1024 * 512 * 128 * 32

BF16 = mybir.dt.bfloat16
F32 = mybir.dt.float32
U32 = mybir.dt.uint32
U8 = mybir.dt.uint8
FP8X4 = mybir.dt.float8_e4m3fn_x4
ADD = mybir.AluOpType.add
IDENTITY = mybir.ActivationFunctionType.Identity

P = 128
PACK = 4
C = 512
T = 128
V = 32
FRAMES = 143
OUT = 1024
PAIRS = V // 2
KA = 8
PITCH = 144
NEED = T + KA
COPIES = 2
LOADS = KA // COPIES
BLOCK = 128
CHUNK = 32
REL_CHUNK = 64
GROUP = 8
QUAD = 4
N_TILE = 512
T_STEP = N_TILE // V


def tile_gccgc_pa_t_kernel(tc, x_pad, rel, A, w3, b3, out):
    nc = tc.nc
    n_groups = C // GROUP
    groups_in_chunk = CHUNK // GROUP
    groups_in_block = BLOCK // GROUP
    n_chunks = C // CHUNK
    run = (CHUNK - 1) * PITCH + NEED

    out_words = out.rearrange("b o t i -> (b o t i)")
    scratch = out_words[0 : PAIRS * COPIES * C * PITCH].rearrange("(blk x) -> blk x", blk=C // BLOCK)
    rel_rows = rel[0].rearrange("(x ka) (jp e) i -> ka jp x (e i)", ka=KA, e=2)

    with ExitStack() as stack:
        keep = stack.enter_context(tc.tile_pool(name="keep", bufs=1))
        sort_pool = stack.enter_context(tc.tile_pool(name="sort", bufs=1))
        win_pool = stack.enter_context(tc.tile_pool(name="win", bufs=2))
        rel_pool = stack.enter_context(tc.tile_pool(name="rel", bufs=2))
        w_pool = stack.enter_context(tc.tile_pool(name="wq", bufs=2))
        x_pool = stack.enter_context(tc.tile_pool(name="xq", bufs=3))
        acc_psum = stack.enter_context(tc.psum_pool(name="acc", bufs=4))
        tr_psum = stack.enter_context(tc.psum_pool(name="tr", bufs=3))
        stack.enter_context(tc.manual_schedule())

        x_rows_of = {}
        frames_of = {}
        raw_of = {}
        w_codes_of = {}
        w_scales_of = {}
        x_in_of = {}
        x_codes_of = {}
        x_scales_of = {}
        acc_of = {}

        def load_block(block):
            x_rows_of[block] = sort_pool.tile([P, FRAMES * V], BF16, name="x_rows")
            nc.sync.dma_start(
                out=x_rows_of[block][:],
                in_=x_pad[0, block * BLOCK : (block + 1) * BLOCK].rearrange("c f v -> c (f v)"),
            )

        def sort_block(block):
            sorted_rows = sort_pool.tile([P, PAIRS, PITCH + LOADS], F32)
            nc.vector.memset(sorted_rows[:, :, FRAMES : PITCH + LOADS], 0.0)
            nc.vector.tensor_copy(
                out=sorted_rows[:, :, 0:FRAMES],
                in_=x_rows_of[block][:].bitcast(F32).rearrange("c (f jp) -> c jp f", jp=PAIRS),
            )
            both = scratch[block].rearrange("(jp s c f) -> s c jp f", jp=PAIRS, s=COPIES, c=BLOCK)
            for s in range(COPIES):
                nc.sync.dma_start(out=both[s], in_=sorted_rows[:, :, LOADS * s : LOADS * s + PITCH])

        def load_frames(chunk):
            frames_of[chunk] = win_pool.tile([P, CHUNK * PITCH], F32, name="frames")
            rows = scratch[chunk * CHUNK // BLOCK].rearrange("(row x) -> row x", row=PAIRS * COPIES)
            for lo in range(LOADS):
                first = (chunk * CHUNK % BLOCK) * PITCH + lo
                nc.scalar.dma_start(out=frames_of[chunk][lo:P:LOADS, 0:run], in_=rows[:, first : first + run])

        def load_rel(part):
            raw_of[part] = rel_pool.tile([P, REL_CHUNK, PACK, V], BF16, name="raw")
            for lo in range(LOADS):
                for queue, ka in ((nc.sync, lo), (nc.gpsimd, lo + LOADS)):
                    queue.dma_start(
                        out=raw_of[part][ka:P:KA].rearrange("p c (kh e) i -> p (c kh) (e i)", e=2),
                        in_=rel_rows[ka, :, 2 * part * REL_CHUNK : 2 * (part + 1) * REL_CHUNK, :],
                    )

        def weights(group):
            chunk = group // groups_in_chunk
            g0 = group % groups_in_chunk * GROUP
            r0 = group * GROUP % REL_CHUNK
            if g0 == 0:
                w_codes_of[chunk] = w_pool.tile([P, CHUNK * V], U32, align_bytes=64, name="w_codes")
                w_scales_of[chunk] = w_pool.tile([P, CHUNK * V], U8, align_bytes=64, name="w_scales")
            w_in = w_pool.tile([P, GROUP, V, PACK], BF16, align_bytes=64)
            nc.vector.tensor_tensor(
                out=w_in[:],
                in0=raw_of[group * GROUP // REL_CHUNK][:, r0 : r0 + GROUP].rearrange("p c r i -> p c i r"),
                in1=a_words[:].rearrange("p i kh e -> p i (kh e)").unsqueeze(1).to_broadcast([P, GROUP, V, PACK]),
                op=ADD,
            )
            cols = slice(g0 * V, (g0 + GROUP) * V)
            nc.vector.quantize_mx(
                out=w_codes_of[chunk][:, cols].bitcast(FP8X4),
                scales=w_scales_of[chunk][:, cols],
                in_=w_in[:].rearrange("p c i r -> p (c i r)"),
            )

        def windows(group):
            g0 = group % groups_in_chunk * GROUP
            blocks = frames_of[group // groups_in_chunk][:].rearrange("p (c u b) -> p c u b", c=CHUNK, b=KA)
            x_in_of[group] = x_pool.tile([P, GROUP * T * PACK], BF16, align_bytes=64, name="x_in")
            words = x_in_of[group][:].bitcast(F32).rearrange(
                "p (c a odd b kh) -> p c a odd b kh", c=GROUP, odd=2, b=KA, kh=2
            )
            for odd in range(2):
                nc.scalar.copy(
                    out=words[:, :, :, odd],
                    in_=blocks[:, g0 : g0 + GROUP, odd : odd + T // KA, :].rearrange(
                        "p c (a kh) b -> p c a b kh", kh=2
                    ),
                )

        def multiply(group):
            x_codes = x_pool.tile([P, GROUP * T], U32, align_bytes=64)
            x_scales = x_pool.tile([P, GROUP * T], U8, align_bytes=64)
            nc.vector.quantize_mx(out=x_codes[:].bitcast(FP8X4), scales=x_scales[:], in_=x_in_of[group][:])
            chunk = group // groups_in_chunk
            for quad in range(GROUP // QUAD):
                q0 = group % groups_in_chunk * GROUP + quad * QUAD
                w_cols = slice(q0 * V, (q0 + QUAD) * V)
                acc = acc_psum.tile([P, QUAD * QUAD * V], F32, tag="acc", name="acc")
                acc_of[(group, quad)] = acc
                for q in range(QUAD):
                    t_cols = slice((quad * QUAD + q) * T, (quad * QUAD + q + 1) * T)
                    nc.tensor.matmul_mx(
                        out=acc[:, q * QUAD * V : (q + 1) * QUAD * V],
                        lhsT=x_codes[:, t_cols].bitcast(FP8X4),
                        lhsT_scale=x_scales[:, t_cols],
                        rhs=w_codes_of[chunk][:, w_cols].bitcast(FP8X4),
                        rhs_scale=w_scales_of[chunk][:, w_cols],
                        start=True,
                        stop=True,
                    )

        def collect(group):
            for quad in range(GROUP // QUAD):
                c0 = group * GROUP + quad * QUAD
                own = acc_of[(group, quad)][:].rearrange("p (blk i) -> p blk i", i=V)[:, 0 : QUAD * QUAD : QUAD + 1, :]
                if group // 2 % 2 == 0:
                    nc.scalar.copy(out=z_sb[:, :, c0 : c0 + QUAD], in_=own.rearrange("p q i -> p i q"))
                else:
                    nc.vector.tensor_copy(out=z_sb[:, :, c0 : c0 + QUAD], in_=own.rearrange("p q i -> p i q"))

        def turn(r):
            for i0 in range(0, V, 8):
                z_ps = tr_psum.tile([P, 8, T], BF16, tag="tr")
                for i in range(8):
                    nc.tensor.transpose(z_ps[:, i, :], z_sb[:, i0 + i, r * P : (r + 1) * P], ident[:])
                if i0 < V // 2:
                    nc.scalar.copy(out=z_t[:, r, :, i0 : i0 + 8], in_=z_ps[:].rearrange("p i t -> p t i"))
                else:
                    nc.vector.tensor_copy(out=z_t[:, r, :, i0 : i0 + 8], in_=z_ps[:].rearrange("p i t -> p t i"))

        load_block(0)
        ident = keep.tile([P, P], BF16)
        make_identity(nc, ident[:])
        a_raw = keep.tile([P, 2, V], BF16)
        for ka in range(KA):
            nc.sync.dma_start(
                out=a_raw[ka:P:KA].rearrange("p e i -> p (e i)"),
                in_=A.rearrange("(jp e) i -> jp (e i)", e=2),
            )
        b3_rows = keep.tile([P, P], BF16)
        nc.vector.memset(b3_rows[:], 0.0)
        nc.sync.dma_start(out=b3_rows[0 : OUT // P, :], in_=b3.rearrange("(a o) -> a o", o=P))
        w3_codes = keep.tile([P, OUT], U32, align_bytes=64)
        w3_scales = keep.tile([P, OUT], U8, align_bytes=64)
        with tc.tile_pool(name="w3", bufs=1) as w3_pool:
            w3_rows = w3_pool.tile([P, OUT // P, C], BF16)
            nc.sync.dma_start(out=w3_rows[:], in_=w3.rearrange("(a p) c -> p a c", p=P))
            load_rel(0)
            sort_block(0)
            load_frames(0)
            load_rel(1)

            b3_ps = tr_psum.tile([P, P], BF16, tag="tr")
            nc.tensor.transpose(b3_ps[:], b3_rows[:], ident[:])
            b3_cols = keep.tile([P, OUT // P], F32)
            nc.vector.tensor_copy(out=b3_cols[:], in_=b3_ps[:, 0 : OUT // P])

            w3_in = w3_pool.tile([P, OUT, PACK], BF16, align_bytes=64)
            for two in range(OUT // P // 2):
                w3_ps = tr_psum.tile([P, 2 * PACK, P], BF16, tag="tr")
                for a in range(2):
                    for r in range(PACK):
                        nc.tensor.transpose(
                            w3_ps[:, a * PACK + r, :], w3_rows[:, 2 * two + a, r * P : (r + 1) * P], ident[:]
                        )
                nc.scalar.copy(
                    out=w3_in[:, 2 * two * P : (2 * two + 2) * P, :].rearrange("p (a o) r -> p a o r", a=2),
                    in_=w3_ps[:].rearrange("p (a r) o -> p a o r", a=2),
                )
            nc.vector.quantize_mx(
                out=w3_codes[:].bitcast(FP8X4),
                scales=w3_scales[:],
                in_=w3_in[:].rearrange("p o r -> p (o r)"),
            )

        a_words = keep.tile([P, V, 2, 2], BF16)
        for kh in range(2):
            nc.vector.tensor_copy(out=a_words[:, :, kh, :], in_=a_raw[:].rearrange("p e i -> p i e"))
        for group in range(groups_in_chunk):
            weights(group)

        late = stack.enter_context(tc.tile_pool(name="late", bufs=1))
        z_pool = stack.enter_context(tc.tile_pool(name="zq", bufs=2))
        y_pool = stack.enter_context(tc.tile_pool(name="y", bufs=4))
        z_sb = keep.tile([P, V, C], BF16)
        z_t = late.tile([P, PACK, T, V], BF16)

        for s in range(n_groups + 3):
            if s % groups_in_chunk == 0:
                chunk = s // groups_in_chunk
                if chunk + 1 < n_chunks:
                    load_frames(chunk + 1)
                if chunk % 2 == 1 and (chunk + 3) // 2 < C // REL_CHUNK:
                    load_rel((chunk + 3) // 2)
            if s % groups_in_block == 0 and s + groups_in_block < n_groups:
                load_block(s // groups_in_block + 1)
            if s < n_groups:
                windows(s)
            if 1 <= s <= n_groups:
                multiply(s - 1)
            if 2 <= s <= n_groups + 1:
                collect(s - 2)
            if s + groups_in_chunk < n_groups:
                weights(s + groups_in_chunk)
            if s % groups_in_block == groups_in_chunk and s + groups_in_block < n_groups:
                sort_block(s // groups_in_block + 1)
            if s >= 3 and (s - 2) % groups_in_block == 0:
                turn((s - 3) // groups_in_block)

        z_codes_of = {}
        z_scales_of = {}

        def quantise_z(step):
            t_rows = slice(step * T_STEP, (step + 1) * T_STEP)
            z_in = z_pool.tile([P, N_TILE, PACK], BF16, align_bytes=64)
            nc.vector.tensor_copy(out=z_in[:], in_=z_t[:, :, t_rows, :].rearrange("p r t i -> p (t i) r"))
            z_codes_of[step] = z_pool.tile([P, N_TILE], U32, align_bytes=64, name="z_codes")
            z_scales_of[step] = z_pool.tile([P, N_TILE], U8, align_bytes=64, name="z_scales")
            nc.vector.quantize_mx(
                out=z_codes_of[step][:].bitcast(FP8X4),
                scales=z_scales_of[step][:],
                in_=z_in[:].rearrange("p n r -> p (n r)"),
            )

        n_steps = T // T_STEP
        quantise_z(0)
        for step in range(n_steps):
            t_rows = slice(step * T_STEP, (step + 1) * T_STEP)
            if step + 1 < n_steps:
                quantise_z(step + 1)
            for a in range(OUT // P):
                o_cols = slice(a * P, (a + 1) * P)
                y_ps = acc_psum.tile([P, N_TILE], F32, tag="acc")
                nc.tensor.matmul_mx(
                    out=y_ps[:],
                    lhsT=w3_codes[:, o_cols].bitcast(FP8X4),
                    lhsT_scale=w3_scales[:, o_cols],
                    rhs=z_codes_of[step][:].bitcast(FP8X4),
                    rhs_scale=z_scales_of[step][:],
                    start=True,
                    stop=True,
                )
                y = y_pool.tile([P, N_TILE], F32)
                if a % 4 == 3:
                    nc.vector.tensor_scalar_add(out=y[:], in0=y_ps[:], scalar1=b3_cols[:, a : a + 1])
                else:
                    nc.scalar.activation(out=y[:], in_=y_ps[:], func=IDENTITY, bias=b3_cols[:, a : a + 1])
                nc.sync.dma_start(out=out[0, o_cols, t_rows, :].rearrange("o t i -> o (t i)"), in_=y[:])
